import numpy as np
import ml_dtypes

BF16 = ml_dtypes.bfloat16


def bf(x):
    return np.asarray(x, np.float32).astype(BF16)


def f32(x):
    return np.asarray(x, np.float32)


def f64(x):
    return np.asarray(x).astype(np.float64)


def striped(idx):
    return np.tile(idx.reshape(-1, 16).T, (8, 1))


C, S, N, D, HALF = 128, 4096, 512, 64, 32
BASE, SCALING, NTK_ALPHA, NTK_BETA, EPS = 150000.0, 32.0, 1.0, 32.0, 1e-5
SWAP = (np.arange(C) + HALF) % D + (np.arange(C) // D) * D


def rope_cache():
    freq = BASE ** (np.arange(HALF, dtype=np.float64) / HALF)
    concentration = 0.1 * np.log(SCALING) + 1.0
    low = HALF * np.log(S / (NTK_BETA * 2 * np.pi)) / np.log(BASE)
    high = HALF * np.log(S / (NTK_ALPHA * 2 * np.pi)) / np.log(BASE)
    ramp = (np.arange(HALF, dtype=np.float64) - low) / (high - low)
    mask = 1.0 - np.clip(ramp, 0.0, 1.0)
    inv_freq = (1.0 / (SCALING * freq)) * (1.0 - mask) + (1.0 / freq) * mask
    ang = np.outer(inv_freq, np.arange(S, dtype=np.float64))
    cos = f32(np.cos(ang) * concentration)
    sin = f32(np.sin(ang) * concentration)
    return np.concatenate([np.tile(np.concatenate([cos, cos]), (C // D, 1)), np.tile(np.concatenate([-sin, sin]), (C // D, 1))])


def setup_inputs():
    z = np.random.standard_normal((C, N))
    x = f32(z * np.sqrt((1.0 - EPS) / np.mean(z * z, axis=0, keepdims=True)))
    return {"x": x, "b": f32(0.1 * np.random.standard_normal((C, 1))), "rope": rope_cache(), "offs": striped(np.random.permutation(np.tile(np.arange(S), 2))[:N])}


def reference(x, b, rope, offs):
    idx = offs[:16].T.reshape(-1)
    y = f64(x) + f64(b)
    r = f64(rope)
    return r[:C][:, idx] * y + r[C:][:, idx] * y[SWAP]

@@ -1,0 +1,49 @@
+import concourse.mybir as mybir
+
+F32 = mybir.dt.float32
+U16 = mybir.dt.uint16
+MULT = mybir.AluOpType.mult
+ADD = mybir.AluOpType.add
+
+CHANNELS = 128
+POSITIONS = 4096
+TOKENS = 512
+HALF = 32
+
+
+def tile_oaiattention_kernel(tc, x, b, rope, offs, out):
+    nc = tc.nc
+    with tc.tile_pool(name="held", bufs=1) as held:
+        offsets = held.tile([CHANNELS, TOKENS // 16], U16, name="offsets")
+        nc.sync.dma_start(offsets[:], offs)
+
+        x_plain = held.tile([CHANNELS, TOKENS], F32, name="x_plain")
+        b_plain = held.tile([CHANNELS, 1], F32, name="b_plain")
+        nc.scalar.dma_start(x_plain[:], x)
+        nc.scalar.dma_start(b_plain[:], b)
+
+        x_swapped = held.tile([CHANNELS, TOKENS], F32, name="x_swapped")
+        b_swapped = held.tile([CHANNELS, 1], F32, name="b_swapped")
+        for block in range(CHANNELS // HALF):
+            here = slice(block * HALF, (block + 1) * HALF)
+            partner = slice((block ^ 1) * HALF, ((block ^ 1) + 1) * HALF)
+            nc.scalar.dma_start(x_swapped[here, :], x[partner, :])
+            nc.scalar.dma_start(b_swapped[here, :], b[partner, :])
+
+        cosines = held.tile([CHANNELS, POSITIONS], F32, name="cosines")
+        sines = held.tile([CHANNELS, POSITIONS], F32, name="sines")
+        nc.sync.dma_start(cosines[:], rope[0:CHANNELS, :])
+        nc.sync.dma_start(sines[:], rope[CHANNELS : 2 * CHANNELS, :])
+
+        y_plain = held.tile([CHANNELS, TOKENS], F32, name="y_plain")
+        y_swapped = held.tile([CHANNELS, TOKENS], F32, name="y_swapped")
+        nc.vector.tensor_scalar_add(y_plain[:], x_plain[:], b_plain[:, 0:1])
+        nc.vector.tensor_scalar_add(y_swapped[:], x_swapped[:], b_swapped[:, 0:1])
+
+        by_cosine = held.tile([CHANNELS, TOKENS], F32, name="by_cosine")
+        by_sine = held.tile([CHANNELS, TOKENS], F32, name="by_sine")
+        rotated = held.tile([CHANNELS, TOKENS], F32, name="rotated")
+        nc.vector.tensor_tensor(by_cosine[:], cosines[:].indirect(offsets[:]), y_plain[:], MULT)
+        nc.vector.tensor_tensor(by_sine[:], sines[:].indirect(offsets[:]), y_swapped[:], MULT)
+        nc.vector.tensor_tensor(rotated[:], by_cosine[:], by_sine[:], ADD)
+        nc.sync.dma_start(out, rotated[:])

@@ -1,4 +1,5 @@
 import concourse.mybir as mybir
+from concourse.masks import make_identity
 
 F32 = mybir.dt.float32
 U16 = mybir.dt.uint16
@@ -13,7 +14,10 @@ HALF = 32
 
 def tile_oaiattention_kernel(tc, x, b, rope, offs, out):
     nc = tc.nc
-    with tc.tile_pool(name="held", bufs=1) as held:
+    with (
+        tc.tile_pool(name="held", bufs=1) as held,
+        tc.psum_pool(name="psum", bufs=1) as psum,
+    ):
         offsets = held.tile([CHANNELS, TOKENS // 16], U16, name="offsets")
         nc.sync.dma_start(offsets[:], offs)
 
@@ -22,23 +26,26 @@ def tile_oaiattention_kernel(tc, x, b, rope, offs, out):
         nc.scalar.dma_start(x_plain[:], x)
         nc.scalar.dma_start(b_plain[:], b)
 
-        x_swapped = held.tile([CHANNELS, TOKENS], F32, name="x_swapped")
-        b_swapped = held.tile([CHANNELS, 1], F32, name="b_swapped")
-        for block in range(CHANNELS // HALF):
-            here = slice(block * HALF, (block + 1) * HALF)
-            partner = slice((block ^ 1) * HALF, ((block ^ 1) + 1) * HALF)
-            nc.scalar.dma_start(x_swapped[here, :], x[partner, :])
-            nc.scalar.dma_start(b_swapped[here, :], b[partner, :])
-
         cosines = held.tile([CHANNELS, POSITIONS], F32, name="cosines")
         sines = held.tile([CHANNELS, POSITIONS], F32, name="sines")
         nc.sync.dma_start(cosines[:], rope[0:CHANNELS, :])
         nc.sync.dma_start(sines[:], rope[CHANNELS : 2 * CHANNELS, :])
 
+        identity = held.tile([CHANNELS, CHANNELS], F32, name="identity")
+        swap_matrix = held.tile([CHANNELS, CHANNELS], F32, name="swap_matrix")
+        make_identity(nc, identity[:])
+        for block in range(CHANNELS // HALF):
+            here = slice(block * HALF, (block + 1) * HALF)
+            partner = slice((block ^ 1) * HALF, ((block ^ 1) + 1) * HALF)
+            nc.vector.tensor_copy(swap_matrix[:, here], identity[:, partner])
+
         y_plain = held.tile([CHANNELS, TOKENS], F32, name="y_plain")
-        y_swapped = held.tile([CHANNELS, TOKENS], F32, name="y_swapped")
         nc.vector.tensor_scalar_add(y_plain[:], x_plain[:], b_plain[:, 0:1])
-        nc.vector.tensor_scalar_add(y_swapped[:], x_swapped[:], b_swapped[:, 0:1])
+
+        y_swapped_psum = psum.tile([CHANNELS, TOKENS], F32, name="y_swapped_psum")
+        y_swapped = held.tile([CHANNELS, TOKENS], F32, name="y_swapped")
+        nc.tensor.matmul(y_swapped_psum[:], swap_matrix[:], y_plain[:], start=True, stop=True)
+        nc.vector.tensor_copy(y_swapped[:], y_swapped_psum[:])
 
         by_cosine = held.tile([CHANNELS, TOKENS], F32, name="by_cosine")
         by_sine = held.tile([CHANNELS, TOKENS], F32, name="by_sine")

@@ -1,5 +1,4 @@
 import concourse.mybir as mybir
-from concourse.masks import make_identity
 
 F32 = mybir.dt.float32
 U16 = mybir.dt.uint16
@@ -23,21 +22,25 @@ def tile_oaiattention_kernel(tc, x, b, rope, offs, out):
 
         x_plain = held.tile([CHANNELS, TOKENS], F32, name="x_plain")
         b_plain = held.tile([CHANNELS, 1], F32, name="b_plain")
-        nc.scalar.dma_start(x_plain[:], x)
         nc.scalar.dma_start(b_plain[:], b)
+        nc.sync.dma_start(x_plain[:], x)
 
         cosines = held.tile([CHANNELS, POSITIONS], F32, name="cosines")
         sines = held.tile([CHANNELS, POSITIONS], F32, name="sines")
         nc.sync.dma_start(cosines[:], rope[0:CHANNELS, :])
         nc.sync.dma_start(sines[:], rope[CHANNELS : 2 * CHANNELS, :])
 
-        identity = held.tile([CHANNELS, CHANNELS], F32, name="identity")
         swap_matrix = held.tile([CHANNELS, CHANNELS], F32, name="swap_matrix")
-        make_identity(nc, identity[:])
-        for block in range(CHANNELS // HALF):
-            here = slice(block * HALF, (block + 1) * HALF)
-            partner = slice((block ^ 1) * HALF, ((block ^ 1) + 1) * HALF)
-            nc.vector.tensor_copy(swap_matrix[:, here], identity[:, partner])
+        nc.gpsimd.memset(swap_matrix[:], 0.0)
+        nc.gpsimd.affine_select(
+            out=swap_matrix[:],
+            in_=swap_matrix[:],
+            pattern=[[-2 * HALF, CHANNELS // (2 * HALF)], [HALF, 2], [-1, HALF]],
+            compare_op=mybir.AluOpType.not_equal,
+            fill=1.0,
+            base=-HALF,
+            channel_multiplier=1,
+        )
 
         y_plain = held.tile([CHANNELS, TOKENS], F32, name="y_plain")
         nc.vector.tensor_scalar_add(y_plain[:], x_plain[:], b_plain[:, 0:1])

@@ -27,8 +27,12 @@ def tile_oaiattention_kernel(tc, x, b, rope, offs, out):
 
         cosines = held.tile([CHANNELS, POSITIONS], F32, name="cosines")
         sines = held.tile([CHANNELS, POSITIONS], F32, name="sines")
-        nc.sync.dma_start(cosines[:], rope[0:CHANNELS, :])
-        nc.sync.dma_start(sines[:], rope[CHANNELS : 2 * CHANNELS, :])
+        left = slice(0, POSITIONS // 2)
+        right = slice(POSITIONS // 2, POSITIONS)
+        nc.sync.dma_start(cosines[:, left], rope[0:CHANNELS, left])
+        nc.scalar.dma_start(cosines[:, right], rope[0:CHANNELS, right])
+        nc.sync.dma_start(sines[:, left], rope[CHANNELS : 2 * CHANNELS, left])
+        nc.scalar.dma_start(sines[:, right], rope[CHANNELS : 2 * CHANNELS, right])
 
         swap_matrix = held.tile([CHANNELS, CHANNELS], F32, name="swap_matrix")
         nc.gpsimd.memset(swap_matrix[:], 0.0)

@@ -8,6 +8,7 @@ ADD = mybir.AluOpType.add
 CHANNELS = 128
 POSITIONS = 4096
 TOKENS = 512
+PIECE = 256
 HALF = 32
 
 
@@ -58,6 +59,11 @@ def tile_oaiattention_kernel(tc, x, b, rope, offs, out):
         by_sine = held.tile([CHANNELS, TOKENS], F32, name="by_sine")
         rotated = held.tile([CHANNELS, TOKENS], F32, name="rotated")
         nc.vector.tensor_tensor(by_cosine[:], cosines[:].indirect(offsets[:]), y_plain[:], MULT)
-        nc.vector.tensor_tensor(by_sine[:], sines[:].indirect(offsets[:]), y_swapped[:], MULT)
-        nc.vector.tensor_tensor(rotated[:], by_cosine[:], by_sine[:], ADD)
-        nc.sync.dma_start(out, rotated[:])
+
+        pieces = [slice(p * PIECE, (p + 1) * PIECE) for p in range(TOKENS // PIECE)]
+        for p, tokens in enumerate(pieces):
+            piece_offsets = offsets[:, p * (PIECE // 16) : (p + 1) * (PIECE // 16)]
+            nc.vector.tensor_tensor(by_sine[:, tokens], sines[:].indirect(piece_offsets), y_swapped[:, tokens], MULT)
+        for tokens in pieces:
+            nc.vector.tensor_tensor(rotated[:, tokens], by_cosine[:, tokens], by_sine[:, tokens], ADD)
+            nc.sync.dma_start(out[:, tokens], rotated[:, tokens])

@@ -24,16 +24,12 @@ def tile_oaiattention_kernel(tc, x, b, rope, offs, out):
         x_plain = held.tile([CHANNELS, TOKENS], F32, name="x_plain")
         b_plain = held.tile([CHANNELS, 1], F32, name="b_plain")
         nc.scalar.dma_start(b_plain[:], b)
-        nc.sync.dma_start(x_plain[:], x)
+        nc.scalar.dma_start(x_plain[:], x)
 
         cosines = held.tile([CHANNELS, POSITIONS], F32, name="cosines")
         sines = held.tile([CHANNELS, POSITIONS], F32, name="sines")
-        left = slice(0, POSITIONS // 2)
-        right = slice(POSITIONS // 2, POSITIONS)
-        nc.sync.dma_start(cosines[:, left], rope[0:CHANNELS, left])
-        nc.scalar.dma_start(cosines[:, right], rope[0:CHANNELS, right])
-        nc.sync.dma_start(sines[:, left], rope[CHANNELS : 2 * CHANNELS, left])
-        nc.scalar.dma_start(sines[:, right], rope[CHANNELS : 2 * CHANNELS, right])
+        nc.sync.dma_start(cosines[:], rope[0:CHANNELS, :])
+        nc.sync.dma_start(sines[:], rope[CHANNELS : 2 * CHANNELS, :])
 
         swap_matrix = held.tile([CHANNELS, CHANNELS], F32, name="swap_matrix")
         nc.gpsimd.memset(swap_matrix[:], 0.0)

@@ -19,17 +19,16 @@ def tile_oaiattention_kernel(tc, x, b, rope, offs, out):
         tc.psum_pool(name="psum", bufs=1) as psum,
     ):
         offsets = held.tile([CHANNELS, TOKENS // 16], U16, name="offsets")
-        nc.sync.dma_start(offsets[:], offs)
-
         x_plain = held.tile([CHANNELS, TOKENS], F32, name="x_plain")
         b_plain = held.tile([CHANNELS, 1], F32, name="b_plain")
-        nc.scalar.dma_start(b_plain[:], b)
-        nc.scalar.dma_start(x_plain[:], x)
-
         cosines = held.tile([CHANNELS, POSITIONS], F32, name="cosines")
         sines = held.tile([CHANNELS, POSITIONS], F32, name="sines")
+
         nc.sync.dma_start(cosines[:], rope[0:CHANNELS, :])
+        nc.sync.dma_start(offsets[:], offs)
         nc.sync.dma_start(sines[:], rope[CHANNELS : 2 * CHANNELS, :])
+        nc.scalar.dma_start(x_plain[:], x)
+        nc.scalar.dma_start(b_plain[:], b)
 
         swap_matrix = held.tile([CHANNELS, CHANNELS], F32, name="swap_matrix")
         nc.gpsimd.memset(swap_matrix[:], 0.0)

@@ -9,6 +9,7 @@ CHANNELS = 128
 POSITIONS = 4096
 TOKENS = 512
 PIECE = 256
+BURST = 256
 HALF = 32
 
 
@@ -21,8 +22,8 @@ def tile_oaiattention_kernel(tc, x, b, rope, offs, out):
         offsets = held.tile([CHANNELS, TOKENS // 16], U16, name="offsets")
         x_plain = held.tile([CHANNELS, TOKENS], F32, name="x_plain")
         b_plain = held.tile([CHANNELS, 1], F32, name="b_plain")
-        cosines = held.tile([CHANNELS, POSITIONS], F32, name="cosines")
-        sines = held.tile([CHANNELS, POSITIONS], F32, name="sines")
+        cosines = held.tile([CHANNELS, POSITIONS], F32, name="cosines", align_bytes=BURST)
+        sines = held.tile([CHANNELS, POSITIONS], F32, name="sines", align_bytes=BURST)
 
         nc.sync.dma_start(cosines[:], rope[0:CHANNELS, :])
         nc.sync.dma_start(offsets[:], offs)

@@ -20,7 +20,7 @@ def tile_oaiattention_kernel(tc, x, b, rope, offs, out):
         tc.psum_pool(name="psum", bufs=1) as psum,
     ):
         offsets = held.tile([CHANNELS, TOKENS // 16], U16, name="offsets")
-        x_plain = held.tile([CHANNELS, TOKENS], F32, name="x_plain")
+        x_plain = held.tile([CHANNELS, TOKENS], F32, name="x_plain", align_bytes=BURST)
         b_plain = held.tile([CHANNELS, 1], F32, name="b_plain")
         cosines = held.tile([CHANNELS, POSITIONS], F32, name="cosines", align_bytes=BURST)
         sines = held.tile([CHANNELS, POSITIONS], F32, name="sines", align_bytes=BURST)
@@ -53,7 +53,7 @@ def tile_oaiattention_kernel(tc, x, b, rope, offs, out):
 
         by_cosine = held.tile([CHANNELS, TOKENS], F32, name="by_cosine")
         by_sine = held.tile([CHANNELS, TOKENS], F32, name="by_sine")
-        rotated = held.tile([CHANNELS, TOKENS], F32, name="rotated")
+        rotated = held.tile([CHANNELS, TOKENS], F32, name="rotated", align_bytes=BURST)
         nc.vector.tensor_tensor(by_cosine[:], cosines[:].indirect(offsets[:]), y_plain[:], MULT)
 
         pieces = [slice(p * PIECE, (p + 1) * PIECE) for p in range(TOKENS // PIECE)]

@@ -21,7 +21,7 @@ def tile_oaiattention_kernel(tc, x, b, rope, offs, out):
     ):
         offsets = held.tile([CHANNELS, TOKENS // 16], U16, name="offsets")
         x_plain = held.tile([CHANNELS, TOKENS], F32, name="x_plain", align_bytes=BURST)
-        b_plain = held.tile([CHANNELS, 1], F32, name="b_plain")
+        b_row = held.tile([1, CHANNELS], F32, name="b_row")
         cosines = held.tile([CHANNELS, POSITIONS], F32, name="cosines", align_bytes=BURST)
         sines = held.tile([CHANNELS, POSITIONS], F32, name="sines", align_bytes=BURST)
 
@@ -29,7 +29,7 @@ def tile_oaiattention_kernel(tc, x, b, rope, offs, out):
         nc.sync.dma_start(offsets[:], offs)
         nc.sync.dma_start(sines[:], rope[CHANNELS : 2 * CHANNELS, :])
         nc.scalar.dma_start(x_plain[:], x)
-        nc.scalar.dma_start(b_plain[:], b)
+        nc.scalar.dma_start(b_row[:], b.rearrange("c o -> o c"))
 
         swap_matrix = held.tile([CHANNELS, CHANNELS], F32, name="swap_matrix")
         nc.gpsimd.memset(swap_matrix[:], 0.0)
@@ -43,8 +43,13 @@ def tile_oaiattention_kernel(tc, x, b, rope, offs, out):
             channel_multiplier=1,
         )
 
+        one = held.tile([1, 1], F32, name="one")
+        nc.vector.memset(one[:], 1.0)
+        b_column = psum.tile([CHANNELS, 1], F32, name="b_column")
+        nc.tensor.matmul(b_column[:], b_row[:], one[:], start=True, stop=True)
+
         y_plain = held.tile([CHANNELS, TOKENS], F32, name="y_plain")
-        nc.vector.tensor_scalar_add(y_plain[:], x_plain[:], b_plain[:, 0:1])
+        nc.vector.tensor_scalar_add(y_plain[:], x_plain[:], b_column[:, 0:1])
 
         y_swapped_psum = psum.tile([CHANNELS, TOKENS], F32, name="y_swapped_psum")
         y_swapped = held.tile([CHANNELS, TOKENS], F32, name="y_swapped")

@@ -8,7 +8,7 @@ ADD = mybir.AluOpType.add
 CHANNELS = 128
 POSITIONS = 4096
 TOKENS = 512
-PIECE = 256
+PIECE_ENDS = (0, 256, 384, 512)
 BURST = 256
 HALF = 32
 
@@ -61,9 +61,9 @@ def tile_oaiattention_kernel(tc, x, b, rope, offs, out):
         rotated = held.tile([CHANNELS, TOKENS], F32, name="rotated", align_bytes=BURST)
         nc.vector.tensor_tensor(by_cosine[:], cosines[:].indirect(offsets[:]), y_plain[:], MULT)
 
-        pieces = [slice(p * PIECE, (p + 1) * PIECE) for p in range(TOKENS // PIECE)]
-        for p, tokens in enumerate(pieces):
-            piece_offsets = offsets[:, p * (PIECE // 16) : (p + 1) * (PIECE // 16)]
+        pieces = [slice(first, last) for first, last in zip(PIECE_ENDS[:-1], PIECE_ENDS[1:])]
+        for tokens in pieces:
+            piece_offsets = offsets[:, tokens.start // 16 : tokens.stop // 16]
             nc.vector.tensor_tensor(by_sine[:, tokens], sines[:].indirect(piece_offsets), y_swapped[:, tokens], MULT)
         for tokens in pieces:
             nc.vector.tensor_tensor(rotated[:, tokens], by_cosine[:, tokens], by_sine[:, tokens], ADD)

@@ -8,9 +8,14 @@ ADD = mybir.AluOpType.add
 CHANNELS = 128
 POSITIONS = 4096
 TOKENS = 512
-PIECE_ENDS = (0, 256, 384, 512)
+PRODUCT_ENDS = (0, 384, 512)
+STORE_ENDS = (0, 192, 384, 512)
 BURST = 256
 HALF = 32
+
+
+def pieces_between(ends):
+    return [slice(first, last) for first, last in zip(ends[:-1], ends[1:])]
 
 
 def tile_oaiattention_kernel(tc, x, b, rope, offs, out):
@@ -61,10 +66,9 @@ def tile_oaiattention_kernel(tc, x, b, rope, offs, out):
         rotated = held.tile([CHANNELS, TOKENS], F32, name="rotated", align_bytes=BURST)
         nc.vector.tensor_tensor(by_cosine[:], cosines[:].indirect(offsets[:]), y_plain[:], MULT)
 
-        pieces = [slice(first, last) for first, last in zip(PIECE_ENDS[:-1], PIECE_ENDS[1:])]
-        for tokens in pieces:
+        for tokens in pieces_between(PRODUCT_ENDS):
             piece_offsets = offsets[:, tokens.start // 16 : tokens.stop // 16]
             nc.vector.tensor_tensor(by_sine[:, tokens], sines[:].indirect(piece_offsets), y_swapped[:, tokens], MULT)
-        for tokens in pieces:
+        for tokens in pieces_between(STORE_ENDS):
             nc.vector.tensor_tensor(rotated[:, tokens], by_cosine[:, tokens], by_sine[:, tokens], ADD)
             nc.sync.dma_start(out[:, tokens], rotated[:, tokens])

@@ -48,18 +48,22 @@ def tile_oaiattention_kernel(tc, x, b, rope, offs, out):
             channel_multiplier=1,
         )
 
+        x_swapped = psum.tile([CHANNELS, TOKENS], F32, name="x_swapped")
+        nc.tensor.matmul(x_swapped[:], swap_matrix[:], x_plain[:], start=True, stop=True)
+
         one = held.tile([1, 1], F32, name="one")
         nc.vector.memset(one[:], 1.0)
-        b_column = psum.tile([CHANNELS, 1], F32, name="b_column")
-        nc.tensor.matmul(b_column[:], b_row[:], one[:], start=True, stop=True)
+        b_column_psum = psum.tile([CHANNELS, 1], F32, name="b_column_psum")
+        b_column = held.tile([CHANNELS, 1], F32, name="b_column")
+        b_swapped = psum.tile([CHANNELS, 1], F32, name="b_swapped")
+        nc.tensor.matmul(b_column_psum[:], b_row[:], one[:], start=True, stop=True)
+        nc.vector.tensor_copy(b_column[:], b_column_psum[:])
+        nc.tensor.matmul(b_swapped[:], swap_matrix[:], b_column[:], start=True, stop=True)
 
         y_plain = held.tile([CHANNELS, TOKENS], F32, name="y_plain")
-        nc.vector.tensor_scalar_add(y_plain[:], x_plain[:], b_column[:, 0:1])
-
-        y_swapped_psum = psum.tile([CHANNELS, TOKENS], F32, name="y_swapped_psum")
         y_swapped = held.tile([CHANNELS, TOKENS], F32, name="y_swapped")
-        nc.tensor.matmul(y_swapped_psum[:], swap_matrix[:], y_plain[:], start=True, stop=True)
-        nc.vector.tensor_copy(y_swapped[:], y_swapped_psum[:])
+        nc.vector.tensor_scalar_add(y_plain[:], x_plain[:], b_column[:, 0:1])
+        nc.vector.tensor_scalar_add(y_swapped[:], x_swapped[:], b_swapped[:, 0:1])
 
         by_cosine = held.tile([CHANNELS, TOKENS], F32, name="by_cosine")
         by_sine = held.tile([CHANNELS, TOKENS], F32, name="by_sine")

import concourse.mybir as mybir

F32 = mybir.dt.float32
U16 = mybir.dt.uint16
MULT = mybir.AluOpType.mult
ADD = mybir.AluOpType.add

CHANNELS = 128
POSITIONS = 4096
TOKENS = 512
PRODUCT_ENDS = (0, 384, 512)
STORE_ENDS = (0, 192, 384, 512)
BURST = 256
HALF = 32


def pieces_between(ends):
    return [slice(first, last) for first, last in zip(ends[:-1], ends[1:])]


def tile_oaiattention_kernel(tc, x, b, rope, offs, out):
    nc = tc.nc
    with (
        tc.tile_pool(name="held", bufs=1) as held,
        tc.psum_pool(name="psum", bufs=1) as psum,
    ):
        offsets = held.tile([CHANNELS, TOKENS // 16], U16, name="offsets")
        x_plain = held.tile([CHANNELS, TOKENS], F32, name="x_plain", align_bytes=BURST)
        b_row = held.tile([1, CHANNELS], F32, name="b_row")
        cosines = held.tile([CHANNELS, POSITIONS], F32, name="cosines", align_bytes=BURST)
        sines = held.tile([CHANNELS, POSITIONS], F32, name="sines", align_bytes=BURST)

        nc.sync.dma_start(cosines[:], rope[0:CHANNELS, :])
        nc.sync.dma_start(offsets[:], offs)
        nc.sync.dma_start(sines[:], rope[CHANNELS : 2 * CHANNELS, :])
        nc.scalar.dma_start(x_plain[:], x)
        nc.scalar.dma_start(b_row[:], b.rearrange("c o -> o c"))

        swap_matrix = held.tile([CHANNELS, CHANNELS], F32, name="swap_matrix")
        nc.gpsimd.memset(swap_matrix[:], 0.0)
        nc.gpsimd.affine_select(
            out=swap_matrix[:],
            in_=swap_matrix[:],
            pattern=[[-2 * HALF, CHANNELS // (2 * HALF)], [HALF, 2], [-1, HALF]],
            compare_op=mybir.AluOpType.not_equal,
            fill=1.0,
            base=-HALF,
            channel_multiplier=1,
        )

        x_swapped = psum.tile([CHANNELS, TOKENS], F32, name="x_swapped")
        nc.tensor.matmul(x_swapped[:], swap_matrix[:], x_plain[:], start=True, stop=True)

        one = held.tile([1, 1], F32, name="one")
        nc.vector.memset(one[:], 1.0)
        b_column_psum = psum.tile([CHANNELS, 1], F32, name="b_column_psum")
        b_column = held.tile([CHANNELS, 1], F32, name="b_column")
        b_swapped = psum.tile([CHANNELS, 1], F32, name="b_swapped")
        nc.tensor.matmul(b_column_psum[:], b_row[:], one[:], start=True, stop=True)
        nc.vector.tensor_copy(b_column[:], b_column_psum[:])
        nc.tensor.matmul(b_swapped[:], swap_matrix[:], b_column[:], start=True, stop=True)

        y_plain = held.tile([CHANNELS, TOKENS], F32, name="y_plain")
        y_swapped = held.tile([CHANNELS, TOKENS], F32, name="y_swapped")
        nc.vector.tensor_scalar_add(y_plain[:], x_plain[:], b_column[:, 0:1])
        nc.vector.tensor_scalar_add(y_swapped[:], x_swapped[:], b_swapped[:, 0:1])

        by_cosine = held.tile([CHANNELS, TOKENS], F32, name="by_cosine")
        by_sine = held.tile([CHANNELS, TOKENS], F32, name="by_sine")
        rotated = held.tile([CHANNELS, TOKENS], F32, name="rotated", align_bytes=BURST)
        nc.vector.tensor_tensor(by_cosine[:], cosines[:].indirect(offsets[:]), y_plain[:], MULT)

        for tokens in pieces_between(PRODUCT_ENDS):
            piece_offsets = offsets[:, tokens.start // 16 : tokens.stop // 16]
            nc.vector.tensor_tensor(by_sine[:, tokens], sines[:].indirect(piece_offsets), y_swapped[:, tokens], MULT)
        for tokens in pieces_between(STORE_ENDS):
            nc.vector.tensor_tensor(rotated[:, tokens], by_cosine[:, tokens], by_sine[:, tokens], ADD)
            nc.sync.dma_start(out[:, tokens], rotated[:, tokens])
